import numpy as np
import ml_dtypes


def mxq(x, axis, fmt="e4m3"):
    dtype, down = {"e4m3": (ml_dtypes.float8_e4m3fn, 7), "e5m2": (ml_dtypes.float8_e5m2, 14)}[fmt]
    v = np.moveaxis(np.asarray(x, np.float32).astype(ml_dtypes.bfloat16).astype(np.float64), axis, -1)
    blocks = v.reshape(v.shape[:-1] + (-1, 32))
    amax = np.abs(blocks).max(-1, keepdims=True)
    byte = np.maximum(np.where(amax > 0, np.frexp(amax)[1] - 1 + 127, 0) - down, 1)
    scale = np.exp2(byte - 127.0)
    codes = (blocks / scale).astype(np.float32).astype(dtype).astype(np.float64)
    return np.moveaxis((codes * scale).reshape(v.shape), -1, axis)


WIDE = False


def mx_kscale(k):
    if not WIDE:
        return np.ones(k)
    levels = np.array([10, -10, 5, -5, 0])
    if k % 512:
        return np.exp2(np.random.permutation(np.resize(levels, k // 32))).repeat(32)
    a = np.empty((k // 512, 16))
    for p in range(k // 512):
        a[p, :8] = np.random.permutation(np.resize(levels, 8))
        for g in range(8):
            far = levels[np.abs(levels - a[p, g]) >= 10]
            a[p, g + 8] = far[np.random.randint(len(far))]
    return np.exp2(a.ravel()).repeat(32)


BF16 = ml_dtypes.bfloat16


def bf(x):
    return np.asarray(x, np.float32).astype(BF16)


def f64(x):
    return np.asarray(x).astype(np.float64)


B, D, HID, G0, RIN, NR = 256, 1024, 2048, 512, 256, 5
EPS = 1e-05
W2S = 0.02


def silu(v):
    return v / (1.0 + np.exp(-v))


def setup_inputs():
    s, t = mx_kscale(G0), mx_kscale(HID)
    return {"x0": bf(np.random.standard_normal((B, G0)) * s),
            "w1_g0": bf(np.random.standard_normal((HID, G0)) / np.sqrt(G0) / s),
            "w3_g0": bf(np.random.standard_normal((HID, G0)) / np.sqrt(G0) / s * t[:, None]),
            "w2_g0": bf(np.random.standard_normal((D, HID)) * W2S / np.sqrt(HID) / t),
            "norm_w": bf(1.0 + 0.1 * np.random.standard_normal(D)),
            "norm_b": bf(0.1 * np.random.standard_normal(D)),
            "term_embed0": bf(np.random.standard_normal(D))}


def reference(x0, w1_g0, w3_g0, w2_g0, norm_w, norm_b, term_embed0):
    xq = mxq(f64(x0), 1, "e4m3")
    gate0 = silu(xq @ mxq(f64(w1_g0), 1, "e4m3").T)
    h = gate0 * (xq @ mxq(f64(w3_g0), 1, "e4m3").T)
    tok = mxq(h, 1, "e4m3") @ mxq(f64(w2_g0), 1, "e4m3").T
    rms = np.sqrt(np.mean(tok * tok, axis=-1, keepdims=True) + EPS)
    return (tok / rms) * f64(norm_w) + f64(norm_b) + f64(term_embed0)

@@ -1,0 +1,289 @@
+from contextlib import ExitStack
+
+import concourse.mybir as mybir
+from concourse.masks import make_identity
+
+F32 = mybir.dt.float32
+BF16 = mybir.dt.bfloat16
+U32 = mybir.dt.uint32
+U8 = mybir.dt.uint8
+FP8X4 = mybir.dt.float8_e4m3fn_x4
+AF = mybir.ActivationFunctionType
+ALU = mybir.AluOpType
+
+TOK, K1, HID, DOUT = 256, 512, 2048, 1024
+EPS = 1e-05
+P = 128
+FLOPS = 2 * TOK * K1 * HID * 2 + 2 * TOK * HID * DOUT
+
+S1_DT = F32
+
+ENG_X = "v"
+ENG_BC = ("a", "a", "a", "v")
+ENG_A = {0: ("a", "v", "a", "v"), 1: ("a", "v", "a", "v"), 2: ("a", "a", "a", "a"), 3: ("a", "a", "a", "a")}
+ENG_C = {0: ("a", "a", "a", "v"), 1: ("a", "a", "a", "v"), 2: ("a", "a", "a", "v"), 3: ("a", "v", "a", "a")}
+ENG_H = {0: "v", 1: "v", 2: "v", 3: "a"}
+
+
+def tile_observationembeddingv2_pa_kernel(tc, x0, w1_g0, w3_g0, w2_g0, norm_w, norm_b, term_embed0, out):
+    nc = tc.nc
+    with ExitStack() as ctx:
+        const = ctx.enter_context(tc.tile_pool(name="const", bufs=1))
+        raw = ctx.enter_context(tc.tile_pool(name="raw", bufs=1))
+        grp = ctx.enter_context(tc.tile_pool(name="grp", bufs=4))
+        mxp = ctx.enter_context(tc.tile_pool(name="mxp", bufs=1))
+        work = ctx.enter_context(tc.tile_pool(name="work", bufs=4))
+        psum = ctx.enter_context(tc.psum_pool(name="psum", bufs=8))
+        ctx.enter_context(tc.manual_schedule())
+
+        neghalf = const.tile([P, 1], F32, name="neghalf")
+        nc.vector.memset(neghalf[:], -0.5)
+        warm = const.tile([P, 1], F32, name="warm")
+        nc.scalar.activation(out=warm[:], in_=neghalf[:], func=AF.Silu)
+        ident = const.tile([P, P], F32, name="ident")
+        make_identity(nc, ident[:])
+        vec_w = const.tile([P, DOUT], BF16, name="vec_w")
+        vec_b = const.tile([P, DOUT], BF16, name="vec_b")
+        ones = const.tile([P, P], BF16, name="ones")
+        nc.vector.memset(vec_w[:], 0.0)
+        nc.vector.memset(vec_b[:], 0.0)
+        nc.vector.memset(ones[:], 1.0)
+
+        w13_raw = {}
+        w2_raw = {}
+
+        def load_w13(g):
+            for nm, src in (("w1", w1_g0), ("w3", w3_g0)):
+                t = raw.tile([P, 4 * K1], BF16, name="%s_raw%d" % (nm, g))
+                nc.sync.dma_start(out=t[:], in_=src[512 * g : 512 * (g + 1), :].rearrange("(p j) k -> p (j k)", j=4))
+                w13_raw[(nm, g)] = t
+
+        def load_w2(q):
+            for i in (2 * q, 2 * q + 1):
+                t = raw.tile([P, HID], BF16, name="w2_raw%d" % i)
+                nc.sync.dma_start(out=t[:], in_=w2_g0[P * i : P * (i + 1), :])
+                w2_raw[i] = t
+
+        x_raw = raw.tile([P, 2 * K1], BF16, name="x_raw")
+        nc.sync.dma_start(out=x_raw[:].rearrange("p (t k) -> p t k", t=2), in_=x0.rearrange("(t p) k -> p t k", p=P))
+        load_w13(0)
+        nc.sync.dma_start(out=vec_w[0:1, :], in_=norm_w.rearrange("(o d) -> o d", o=1))
+        nc.sync.dma_start(out=vec_b[0:1, :], in_=norm_b.rearrange("(o d) -> o d", o=1))
+        nc.sync.dma_start(out=vec_b[1:2, :], in_=term_embed0.rearrange("(o d) -> o d", o=1))
+        load_w13(1)
+        load_w2(0)
+        load_w13(2)
+        load_w2(1)
+        load_w13(3)
+        load_w2(2)
+        load_w2(3)
+
+        def new_bank(dtype):
+            bank = psum.tile([P, 512], dtype, tag="bank", name="bank")
+            return bank
+
+        def move(eng, dst, src):
+            if eng == "a":
+                nc.scalar.copy(out=dst, in_=src)
+            else:
+                nc.vector.tensor_copy(out=dst, in_=src)
+
+        def quantize(grouped, codes, scales):
+            nc.vector.quantize_mx(out=codes.bitcast(FP8X4), scales=scales, in_=grouped)
+
+        def mx(acc, lc, ls, rc, rs, start, stop):
+            nc.tensor.matmul_mx(out=acc, lhsT=lc.bitcast(FP8X4), lhsT_scale=ls, rhs=rc.bitcast(FP8X4), rhs_scale=rs, start=start, stop=stop)
+
+        def pair_bank(word_views, eng, name):
+            bank = new_bank(F32)
+            for u in range(2):
+                for t in range(2):
+                    s = 2 * u + t
+                    nc.tensor.transpose(out=bank[:, P * s : P * (s + 1)], in_=word_views[t][u], identity=ident[:])
+            grouped = grp.tile([P, 1024], BF16, tag="g1024", name=name, align_bytes=64, bufs=6)
+            move(eng, grouped[:].bitcast(F32).rearrange("p (c u) -> p c u", u=2), bank[:].rearrange("p (u c) -> p c u", u=2))
+            return grouped
+
+        x_codes = mxp.tile([P, TOK], U32, name="x_codes", align_bytes=64)
+        x_scales = mxp.tile([P, TOK], U8, name="x_scales", align_bytes=64)
+        xw = x_raw[:].bitcast(F32)
+        gx = pair_bank([[xw[:, 256 * t + u : 256 * (t + 1) : 2] for u in range(2)] for t in range(2)], ENG_X, "gx")
+        quantize(gx[:], x_codes[:], x_scales[:])
+
+        w13_grouped = {}
+        w13_codes = {}
+        w13_scales = {}
+
+        def a_bank(nm, g, jh, eng):
+            words = w13_raw[(nm, g)][:].bitcast(F32)
+            if jh == 0:
+                w13_grouped[(nm, g)] = grp.tile([P, 2048], BF16, tag="g2048", name="gw", align_bytes=64, bufs=4)
+            grouped = w13_grouped[(nm, g)]
+            bank = new_bank(F32)
+            for e in range(2):
+                for u in range(2):
+                    j = 2 * jh + e
+                    s = 2 * e + u
+                    nc.tensor.transpose(out=bank[:, P * s : P * (s + 1)], in_=words[:, 256 * j + u : 256 * (j + 1) : 2], identity=ident[:])
+            move(
+                eng,
+                grouped[:, 1024 * jh : 1024 * (jh + 1)].bitcast(F32).rearrange("p (r s) -> p r s", s=4),
+                bank[:].rearrange("p (s r) -> p r s", s=4),
+            )
+
+        def a_quant(nm, g):
+            codes = mxp.tile([P, 512], U32, name="%s_codes%d" % (nm, g), align_bytes=64)
+            scales = mxp.tile([P, 512], U8, name="%s_scales%d" % (nm, g), align_bytes=64)
+            quantize(w13_grouped[(nm, g)][:], codes[:], scales[:])
+            w13_codes[(nm, g)] = codes
+            w13_scales[(nm, g)] = scales
+
+        bc = {}
+
+        def block_bc():
+            i = 0
+            for nm, vec in (("w", vec_w), ("b", vec_b)):
+                for nb in range(2):
+                    bank = new_bank(F32)
+                    nc.tensor.matmul(out=bank[:], lhsT=ones[:], rhs=vec[:, 512 * nb : 512 * (nb + 1)], start=True, stop=True)
+                    t = const.tile([P, 512], F32, name="bc_%s%d" % (nm, nb))
+                    move(ENG_BC[i], t[:], bank[:])
+                    bc[(nm, nb)] = t
+                    i += 1
+
+        w2_grouped = {}
+        w2_codes = {}
+        w2_scales = {}
+        for g in range(4):
+            for nb in range(2):
+                w2_codes[(g, nb)] = mxp.tile([P, 512], U32, name="w2_codes%d_%d" % (g, nb), align_bytes=64)
+                w2_scales[(g, nb)] = mxp.tile([P, 512], U8, name="w2_scales%d_%d" % (g, nb), align_bytes=64)
+
+        def c_bank(q, g, eng):
+            views = [w2_raw[2 * q + il][:].bitcast(F32) for il in range(2)]
+            w2_grouped[(q, g)] = pair_bank([[v[:, 256 * g + u : 256 * (g + 1) : 2] for u in range(2)] for v in views], eng, "g2")
+
+        def c_quant(q, g):
+            cols = slice(256 * (q % 2), 256 * (q % 2) + 256)
+            quantize(w2_grouped[(q, g)][:], w2_codes[(g, q // 2)][:, cols], w2_scales[(g, q // 2)][:, cols])
+
+        s1 = {}
+
+        def first_product(g, nm):
+            for tt in range(2):
+                bank = new_bank(S1_DT)
+                cols = slice(P * tt, P * (tt + 1))
+                mx(bank[:], x_codes[:, cols], x_scales[:, cols], w13_codes[(nm, g)][:], w13_scales[(nm, g)][:], True, True)
+                s1[(nm, g, tt)] = bank
+
+        gate = {}
+        hid = {}
+
+        def silu(g, tt):
+            t = work.tile([P, 512], F32, tag="gate", name="gate", bufs=4)
+            nc.scalar.activation(out=t[:], in_=s1[("w1", g, tt)][:], func=AF.Silu)
+            gate[(g, tt)] = t
+
+        def mult(g, tt):
+            t = work.tile([P, 512], BF16, name="hid%d_%d" % (g, tt), bufs=1)
+            nc.vector.tensor_tensor(out=t[:], in0=s1[("w3", g, tt)][:], in1=gate[(g, tt)][:], op=ALU.mult)
+            hid[(g, tt)] = t
+
+        h_grouped = {}
+        h_codes = {}
+        h_scales = {}
+
+        def h_bank(g, eng):
+            views = [hid[(g, tt)][:].bitcast(F32) for tt in range(2)]
+            h_grouped[g] = pair_bank([[v[:, P * u : P * (u + 1)] for u in range(2)] for v in views], eng, "gh")
+
+        def h_quant(g):
+            h_codes[g] = mxp.tile([P, TOK], U32, name="h_codes%d" % g, align_bytes=64)
+            h_scales[g] = mxp.tile([P, TOK], U8, name="h_scales%d" % g, align_bytes=64)
+            quantize(h_grouped[g][:], h_codes[g][:], h_scales[g][:])
+
+        for g in range(2):
+            for wi, nm in enumerate(("w1", "w3")):
+                a_bank(nm, g, 0, ENG_A[g][2 * wi])
+                a_bank(nm, g, 1, ENG_A[g][2 * wi + 1])
+                a_quant(nm, g)
+            if g == 0:
+                block_bc()
+        for r in range(4):
+            first_product(r, "w1")
+            silu(r, 0)
+            silu(r, 1)
+            if r in (1, 2):
+                a_bank("w1", r + 1, 0, ENG_A[r + 1][0])
+                a_bank("w1", r + 1, 1, ENG_A[r + 1][1])
+                a_quant("w1", r + 1)
+                a_bank("w3", r + 1, 0, ENG_A[r + 1][2])
+                a_bank("w3", r + 1, 1, ENG_A[r + 1][3])
+            first_product(r, "w3")
+            mult(r, 0)
+            if r in (1, 2):
+                a_quant("w3", r + 1)
+            mult(r, 1)
+            c_bank(r, 0, ENG_C[r][0])
+            c_bank(r, 1, ENG_C[r][1])
+            c_quant(r, 0)
+            c_bank(r, 2, ENG_C[r][2])
+            c_quant(r, 1)
+            c_bank(r, 3, ENG_C[r][3])
+            c_quant(r, 2)
+            h_bank(r, ENG_H[r])
+            c_quant(r, 3)
+            h_quant(r)
+
+        acc = {}
+
+        def s2(tt, nb, g):
+            if g == 0:
+                acc[(tt, nb)] = new_bank(F32)
+            cols = slice(P * tt, P * (tt + 1))
+            mx(acc[(tt, nb)][:], h_codes[g][:, cols], h_scales[g][:, cols], w2_codes[(g, nb)][:], w2_scales[(g, nb)][:], g == 0, g == 3)
+
+        sumsq = {}
+        scaled = {}
+        for tt in range(2):
+            sumsq[tt] = const.tile([P, 2], F32, name="sumsq%d" % tt)
+
+        def square(tt, nb):
+            junk = work.tile([P, 512], BF16, tag="junk", name="junk", bufs=2)
+            nc.scalar.activation(out=junk[:], in_=acc[(tt, nb)][:], func=AF.Square, scale=1.0 / 32.0, accum_out=sumsq[tt][:, nb : nb + 1])
+
+        def gain(tt, nb):
+            t = work.tile([P, 512], F32, name="scaled%d_%d" % (tt, nb), bufs=1)
+            nc.vector.tensor_tensor(out=t[:], in0=acc[(tt, nb)][:], in1=bc[("w", nb)][:], op=ALU.mult)
+            scaled[(tt, nb)] = t
+
+        rstd = {}
+
+        def inv_rms(tt):
+            ms = const.tile([P, 1], F32, name="ms%d" % tt)
+            nc.gpsimd.tensor_scalar(out=ms[:], in0=sumsq[tt][:, 0:1], scalar1=sumsq[tt][:, 1:2], scalar2=EPS, op0=ALU.add, op1=ALU.add)
+            rstd[tt] = const.tile([P, 1], F32, name="rstd%d" % tt)
+            nc.gpsimd.tensor_tensor(out=rstd[tt][:], in0=ms[:], in1=neghalf[:], op=ALU.pow)
+
+        def finish(tt, nb):
+            o = work.tile([P, 512], F32, name="o%d_%d" % (tt, nb), bufs=1)
+            nc.vector.scalar_tensor_tensor(out=o[:], in0=scaled[(tt, nb)][:], scalar=rstd[tt][:, 0:1], in1=bc[("b", nb)][:], op0=ALU.mult, op1=ALU.add)
+            nc.sync.dma_start(out=out[P * tt : P * (tt + 1), 512 * nb : 512 * (nb + 1)], in_=o[:])
+
+        for nb in range(2):
+            for g in range(3):
+                s2(0, nb, g)
+        s2(0, 0, 3)
+        s2(0, 1, 3)
+        for tt in range(2):
+            if tt == 1:
+                for nb in range(2):
+                    for g in range(4):
+                        s2(1, nb, g)
+            square(tt, 0)
+            square(tt, 1)
+            gain(tt, 0)
+            gain(tt, 1)
+            inv_rms(tt)
+            finish(tt, 0)
+            finish(tt, 1)

@@ -11,18 +11,19 @@ FP8X4 = mybir.dt.float8_e4m3fn_x4
 AF = mybir.ActivationFunctionType
 ALU = mybir.AluOpType
 
-TOK, K1, HID, DOUT = 256, 512, 2048, 1024
+TOKENS, K_IN, HIDDEN, D_OUT = 256, 512, 2048, 1024
 EPS = 1e-05
+FLOPS = 2 * TOKENS * K_IN * HIDDEN * 2 + 2 * TOKENS * HIDDEN * D_OUT
+
 P = 128
-FLOPS = 2 * TOK * K1 * HID * 2 + 2 * TOK * HID * DOUT
+K_PASS = 512
+N_BANK = 512
+WORDS = K_PASS // 2
+GROUPS = HIDDEN // K_PASS
+TOKEN_TILES = TOKENS // P
+OUT_BANKS = D_OUT // N_BANK
 
-S1_DT = F32
-
-ENG_X = "v"
-ENG_BC = ("a", "a", "a", "v")
-ENG_A = {0: ("a", "v", "a", "v"), 1: ("a", "v", "a", "v"), 2: ("a", "a", "a", "a"), 3: ("a", "a", "a", "a")}
-ENG_C = {0: ("a", "a", "a", "v"), 1: ("a", "a", "a", "v"), 2: ("a", "a", "a", "v"), 3: ("a", "v", "a", "a")}
-ENG_H = {0: "v", 1: "v", 2: "v", 3: "a"}
+FIRST_PRODUCT_PSUM = F32
 
 
 def tile_observationembeddingv2_pa_kernel(tc, x0, w1_g0, w3_g0, w2_g0, norm_w, norm_b, term_embed0, out):
@@ -42,248 +43,170 @@ def tile_observationembeddingv2_pa_kernel(tc, x0, w1_g0, w3_g0, w2_g0, norm_w, n
         nc.scalar.activation(out=warm[:], in_=neghalf[:], func=AF.Silu)
         ident = const.tile([P, P], F32, name="ident")
         make_identity(nc, ident[:])
-        vec_w = const.tile([P, DOUT], BF16, name="vec_w")
-        vec_b = const.tile([P, DOUT], BF16, name="vec_b")
-        ones = const.tile([P, P], BF16, name="ones")
-        nc.vector.memset(vec_w[:], 0.0)
-        nc.vector.memset(vec_b[:], 0.0)
-        nc.vector.memset(ones[:], 1.0)
 
-        w13_raw = {}
-        w2_raw = {}
-
-        def load_w13(g):
-            for nm, src in (("w1", w1_g0), ("w3", w3_g0)):
-                t = raw.tile([P, 4 * K1], BF16, name="%s_raw%d" % (nm, g))
-                nc.sync.dma_start(out=t[:], in_=src[512 * g : 512 * (g + 1), :].rearrange("(p j) k -> p (j k)", j=4))
-                w13_raw[(nm, g)] = t
-
-        def load_w2(q):
-            for i in (2 * q, 2 * q + 1):
-                t = raw.tile([P, HID], BF16, name="w2_raw%d" % i)
-                nc.sync.dma_start(out=t[:], in_=w2_g0[P * i : P * (i + 1), :])
-                w2_raw[i] = t
-
-        x_raw = raw.tile([P, 2 * K1], BF16, name="x_raw")
-        nc.sync.dma_start(out=x_raw[:].rearrange("p (t k) -> p t k", t=2), in_=x0.rearrange("(t p) k -> p t k", p=P))
-        load_w13(0)
-        nc.sync.dma_start(out=vec_w[0:1, :], in_=norm_w.rearrange("(o d) -> o d", o=1))
-        nc.sync.dma_start(out=vec_b[0:1, :], in_=norm_b.rearrange("(o d) -> o d", o=1))
-        nc.sync.dma_start(out=vec_b[1:2, :], in_=term_embed0.rearrange("(o d) -> o d", o=1))
-        load_w13(1)
-        load_w2(0)
-        load_w13(2)
-        load_w2(1)
-        load_w13(3)
-        load_w2(2)
-        load_w2(3)
+        weights = {"w1": w1_g0, "w3": w3_g0}
+        w13_words = {}
+        for nm in ("w1", "w3"):
+            rows = weights[nm][0:K_PASS, :].rearrange("(p j) k -> p j k", j=4)
+            for half in range(2):
+                t = raw.tile([P, 2 * K_IN], BF16, name="%s_raw0_%d" % (nm, half))
+                nc.sync.dma_start(out=t[:].rearrange("p (j k) -> p j k", j=2), in_=rows[:, 2 * half : 2 * half + 2, :])
+                w13_words[(nm, 0, half)] = t[:].bitcast(F32)
+        x_raw = raw.tile([P, TOKEN_TILES * K_IN], BF16, name="x_raw")
+        nc.sync.dma_start(out=x_raw[:].rearrange("p (t k) -> p t k", t=TOKEN_TILES), in_=x0.rearrange("(t p) k -> p t k", p=P))
+        for g in range(1, GROUPS):
+            for nm in ("w1", "w3"):
+                t = raw.tile([P, 4 * K_IN], BF16, name="%s_raw%d" % (nm, g))
+                nc.sync.dma_start(out=t[:], in_=weights[nm][K_PASS * g : K_PASS * (g + 1), :].rearrange("(p j) k -> p (j k)", j=4))
+                for half in range(2):
+                    w13_words[(nm, g, half)] = t[:].bitcast(F32)[:, 2 * WORDS * half : 2 * WORDS * (half + 1)]
+        w2_words = []
+        for i in range(D_OUT // P):
+            t = raw.tile([P, HIDDEN], BF16, name="w2_raw%d" % i)
+            nc.sync.dma_start(out=t[:], in_=w2_g0[P * i : P * (i + 1), :])
+            w2_words.append(t[:].bitcast(F32))
+        spread = {}
+        for nm, vec in (("norm_w", norm_w), ("norm_b", norm_b), ("term", term_embed0)):
+            spread[nm] = const.tile([P, D_OUT], BF16, name="spread_%s" % nm)
+            nc.sync.dma_start(out=spread[nm][:], in_=vec.partition_broadcast(P))
 
         def new_bank(dtype):
-            bank = psum.tile([P, 512], dtype, tag="bank", name="bank")
+            bank = psum.tile([P, N_BANK], dtype, tag="bank", name="bank")
             return bank
 
-        def move(eng, dst, src):
-            if eng == "a":
-                nc.scalar.copy(out=dst, in_=src)
-            else:
+        emptied = []
+
+        def empty_bank(dst, src):
+            if len(emptied) % 4 == 3:
                 nc.vector.tensor_copy(out=dst, in_=src)
+            else:
+                nc.scalar.copy(out=dst, in_=src)
+            emptied.append(1)
 
-        def quantize(grouped, codes, scales):
-            nc.vector.quantize_mx(out=codes.bitcast(FP8X4), scales=scales, in_=grouped)
+        waiting = []
 
-        def mx(acc, lc, ls, rc, rs, start, stop):
-            nc.tensor.matmul_mx(out=acc, lhsT=lc.bitcast(FP8X4), lhsT_scale=ls, rhs=rc.bitcast(FP8X4), rhs_scale=rs, start=start, stop=stop)
+        def quantize_waiting():
+            while len(waiting) > 0:
+                grouped, codes, scales = waiting.pop(0)
+                nc.vector.quantize_mx(out=codes.bitcast(FP8X4), scales=scales, in_=grouped)
 
-        def pair_bank(word_views, eng, name):
+        def turn(word_slices, grouped_words, order):
             bank = new_bank(F32)
-            for u in range(2):
-                for t in range(2):
-                    s = 2 * u + t
-                    nc.tensor.transpose(out=bank[:, P * s : P * (s + 1)], in_=word_views[t][u], identity=ident[:])
-            grouped = grp.tile([P, 1024], BF16, tag="g1024", name=name, align_bytes=64, bufs=6)
-            move(eng, grouped[:].bitcast(F32).rearrange("p (c u) -> p c u", u=2), bank[:].rearrange("p (u c) -> p c u", u=2))
-            return grouped
+            for s in range(4):
+                nc.tensor.transpose(out=bank[:, P * s : P * (s + 1)], in_=word_slices[s], identity=ident[:])
+            if order == "row major":
+                empty_bank(grouped_words.rearrange("p (r s) -> p r s", s=4), bank[:].rearrange("p (s r) -> p r s", s=4))
+            else:
+                empty_bank(grouped_words.rearrange("p (c u) -> p c u", u=2), bank[:].rearrange("p (u c) -> p c u", u=2))
+            quantize_waiting()
 
-        x_codes = mxp.tile([P, TOK], U32, name="x_codes", align_bytes=64)
-        x_scales = mxp.tile([P, TOK], U8, name="x_scales", align_bytes=64)
-        xw = x_raw[:].bitcast(F32)
-        gx = pair_bank([[xw[:, 256 * t + u : 256 * (t + 1) : 2] for u in range(2)] for t in range(2)], ENG_X, "gx")
-        quantize(gx[:], x_codes[:], x_scales[:])
+        def turn_pair(views, step, start, codes, scales, name):
+            grouped = grp.tile([P, 4 * 2 * P], BF16, tag="g1024", name=name, align_bytes=64, bufs=6)
+            if step == 2:
+                slices = [views[t][:, start + u : start + WORDS : 2] for u in range(2) for t in range(2)]
+            else:
+                slices = [views[t][:, start + P * u : start + P * (u + 1)] for u in range(2) for t in range(2)]
+            turn(slices, grouped[:].bitcast(F32), "column major")
+            waiting.append((grouped[:], codes, scales))
 
-        w13_grouped = {}
-        w13_codes = {}
-        w13_scales = {}
-
-        def a_bank(nm, g, jh, eng):
-            words = w13_raw[(nm, g)][:].bitcast(F32)
-            if jh == 0:
-                w13_grouped[(nm, g)] = grp.tile([P, 2048], BF16, tag="g2048", name="gw", align_bytes=64, bufs=4)
-            grouped = w13_grouped[(nm, g)]
-            bank = new_bank(F32)
-            for e in range(2):
-                for u in range(2):
-                    j = 2 * jh + e
-                    s = 2 * e + u
-                    nc.tensor.transpose(out=bank[:, P * s : P * (s + 1)], in_=words[:, 256 * j + u : 256 * (j + 1) : 2], identity=ident[:])
-            move(
-                eng,
-                grouped[:, 1024 * jh : 1024 * (jh + 1)].bitcast(F32).rearrange("p (r s) -> p r s", s=4),
-                bank[:].rearrange("p (s r) -> p r s", s=4),
+        def matmul_mx(acc, lhs, lhs_cols, rhs, start, stop):
+            nc.tensor.matmul_mx(
+                out=acc,
+                lhsT=lhs[0][:, lhs_cols].bitcast(FP8X4),
+                lhsT_scale=lhs[1][:, lhs_cols],
+                rhs=rhs[0][:].bitcast(FP8X4),
+                rhs_scale=rhs[1][:],
+                start=start,
+                stop=stop,
             )
 
-        def a_quant(nm, g):
-            codes = mxp.tile([P, 512], U32, name="%s_codes%d" % (nm, g), align_bytes=64)
-            scales = mxp.tile([P, 512], U8, name="%s_scales%d" % (nm, g), align_bytes=64)
-            quantize(w13_grouped[(nm, g)][:], codes[:], scales[:])
-            w13_codes[(nm, g)] = codes
-            w13_scales[(nm, g)] = scales
+        def mx_tiles(width, name):
+            codes = mxp.tile([P, width], U32, name="%s_codes" % name, align_bytes=64)
+            scales = mxp.tile([P, width], U8, name="%s_scales" % name, align_bytes=64)
+            return (codes, scales)
 
-        bc = {}
+        x_mx = mx_tiles(TOKENS, "x")
+        w13_mx = {}
 
-        def block_bc():
-            i = 0
-            for nm, vec in (("w", vec_w), ("b", vec_b)):
-                for nb in range(2):
-                    bank = new_bank(F32)
-                    nc.tensor.matmul(out=bank[:], lhsT=ones[:], rhs=vec[:, 512 * nb : 512 * (nb + 1)], start=True, stop=True)
-                    t = const.tile([P, 512], F32, name="bc_%s%d" % (nm, nb))
-                    move(ENG_BC[i], t[:], bank[:])
-                    bc[(nm, nb)] = t
-                    i += 1
+        def turn_w13(g):
+            for nm in ("w1", "w3"):
+                grouped = grp.tile([P, 4 * N_BANK], BF16, tag="g2048", name="gw", align_bytes=64, bufs=4)
+                for half in range(2):
+                    words = w13_words[(nm, g, half)]
+                    slices = [words[:, WORDS * e + u : WORDS * (e + 1) : 2] for e in range(2) for u in range(2)]
+                    turn(slices, grouped[:, 2 * N_BANK * half : 2 * N_BANK * (half + 1)].bitcast(F32), "row major")
+                w13_mx[(nm, g)] = mx_tiles(N_BANK, "%s_%d" % (nm, g))
+                waiting.append((grouped[:], w13_mx[(nm, g)][0][:], w13_mx[(nm, g)][1][:]))
 
-        w2_grouped = {}
-        w2_codes = {}
-        w2_scales = {}
-        for g in range(4):
-            for nb in range(2):
-                w2_codes[(g, nb)] = mxp.tile([P, 512], U32, name="w2_codes%d_%d" % (g, nb), align_bytes=64)
-                w2_scales[(g, nb)] = mxp.tile([P, 512], U8, name="w2_scales%d_%d" % (g, nb), align_bytes=64)
+        turn_w13(0)
+        xw = x_raw[:].bitcast(F32)
+        turn_pair([xw[:, WORDS * t : WORDS * (t + 1)] for t in range(TOKEN_TILES)], 2, 0, x_mx[0][:], x_mx[1][:], "gx")
+        for g in range(1, GROUPS):
+            turn_w13(g)
+        quantize_waiting()
 
-        def c_bank(q, g, eng):
-            views = [w2_raw[2 * q + il][:].bitcast(F32) for il in range(2)]
-            w2_grouped[(q, g)] = pair_bank([[v[:, 256 * g + u : 256 * (g + 1) : 2] for u in range(2)] for v in views], eng, "g2")
+        hidden = {}
+        for g in range(GROUPS):
+            banks = {}
+            gates = {}
+            for nm in ("w1", "w3"):
+                for tt in range(TOKEN_TILES):
+                    banks[(nm, tt)] = new_bank(FIRST_PRODUCT_PSUM)
+                    matmul_mx(banks[(nm, tt)][:], x_mx, slice(P * tt, P * (tt + 1)), w13_mx[(nm, g)], True, True)
+                for tt in range(TOKEN_TILES):
+                    if nm == "w1":
+                        gates[tt] = work.tile([P, N_BANK], F32, tag="gate", name="gate", bufs=4)
+                        nc.scalar.activation(out=gates[tt][:], in_=banks[(nm, tt)][:], func=AF.Silu)
+                    else:
+                        hidden[(g, tt)] = work.tile([P, N_BANK], BF16, name="hid%d_%d" % (g, tt), bufs=1)
+                        nc.vector.tensor_tensor(out=hidden[(g, tt)][:], in0=banks[(nm, tt)][:], in1=gates[tt][:], op=ALU.mult)
 
-        def c_quant(q, g):
-            cols = slice(256 * (q % 2), 256 * (q % 2) + 256)
-            quantize(w2_grouped[(q, g)][:], w2_codes[(g, q // 2)][:, cols], w2_scales[(g, q // 2)][:, cols])
+        h_mx = {}
+        w2_mx = {}
+        for g in range(GROUPS):
+            for nb in range(OUT_BANKS):
+                w2_mx[(g, nb)] = mx_tiles(N_BANK, "w2_%d_%d" % (g, nb))
 
-        s1 = {}
+        def turn_hidden(g):
+            h_mx[g] = mx_tiles(TOKENS, "h_%d" % g)
+            turn_pair([hidden[(g, tt)][:].bitcast(F32) for tt in range(TOKEN_TILES)], 1, 0, h_mx[g][0][:], h_mx[g][1][:], "gh")
 
-        def first_product(g, nm):
-            for tt in range(2):
-                bank = new_bank(S1_DT)
-                cols = slice(P * tt, P * (tt + 1))
-                mx(bank[:], x_codes[:, cols], x_scales[:, cols], w13_codes[(nm, g)][:], w13_scales[(nm, g)][:], True, True)
-                s1[(nm, g, tt)] = bank
+        def turn_w2(q):
+            cols = slice(2 * P * (q % 2), 2 * P * (q % 2 + 1))
+            for g in range(GROUPS):
+                dst = w2_mx[(g, q // 2)]
+                turn_pair(w2_words[2 * q : 2 * q + 2], 2, WORDS * g, dst[0][:, cols], dst[1][:, cols], "g2")
 
-        gate = {}
-        hid = {}
+        for g in range(GROUPS - 1):
+            turn_hidden(g)
+        turn_w2(0)
+        turn_hidden(GROUPS - 1)
+        for q in range(1, 4):
+            turn_w2(q)
+        quantize_waiting()
 
-        def silu(g, tt):
-            t = work.tile([P, 512], F32, tag="gate", name="gate", bufs=4)
-            nc.scalar.activation(out=t[:], in_=s1[("w1", g, tt)][:], func=AF.Silu)
-            gate[(g, tt)] = t
+        bias = []
+        for nb in range(OUT_BANKS):
+            cols = slice(N_BANK * nb, N_BANK * (nb + 1))
+            bias.append(const.tile([P, N_BANK], F32, name="bias%d" % nb))
+            nc.vector.tensor_tensor(out=bias[nb][:], in0=spread["norm_b"][:, cols], in1=spread["term"][:, cols], op=ALU.add)
 
-        def mult(g, tt):
-            t = work.tile([P, 512], BF16, name="hid%d_%d" % (g, tt), bufs=1)
-            nc.vector.tensor_tensor(out=t[:], in0=s1[("w3", g, tt)][:], in1=gate[(g, tt)][:], op=ALU.mult)
-            hid[(g, tt)] = t
-
-        h_grouped = {}
-        h_codes = {}
-        h_scales = {}
-
-        def h_bank(g, eng):
-            views = [hid[(g, tt)][:].bitcast(F32) for tt in range(2)]
-            h_grouped[g] = pair_bank([[v[:, P * u : P * (u + 1)] for u in range(2)] for v in views], eng, "gh")
-
-        def h_quant(g):
-            h_codes[g] = mxp.tile([P, TOK], U32, name="h_codes%d" % g, align_bytes=64)
-            h_scales[g] = mxp.tile([P, TOK], U8, name="h_scales%d" % g, align_bytes=64)
-            quantize(h_grouped[g][:], h_codes[g][:], h_scales[g][:])
-
-        for g in range(2):
-            for wi, nm in enumerate(("w1", "w3")):
-                a_bank(nm, g, 0, ENG_A[g][2 * wi])
-                a_bank(nm, g, 1, ENG_A[g][2 * wi + 1])
-                a_quant(nm, g)
-            if g == 0:
-                block_bc()
-        for r in range(4):
-            first_product(r, "w1")
-            silu(r, 0)
-            silu(r, 1)
-            if r in (1, 2):
-                a_bank("w1", r + 1, 0, ENG_A[r + 1][0])
-                a_bank("w1", r + 1, 1, ENG_A[r + 1][1])
-                a_quant("w1", r + 1)
-                a_bank("w3", r + 1, 0, ENG_A[r + 1][2])
-                a_bank("w3", r + 1, 1, ENG_A[r + 1][3])
-            first_product(r, "w3")
-            mult(r, 0)
-            if r in (1, 2):
-                a_quant("w3", r + 1)
-            mult(r, 1)
-            c_bank(r, 0, ENG_C[r][0])
-            c_bank(r, 1, ENG_C[r][1])
-            c_quant(r, 0)
-            c_bank(r, 2, ENG_C[r][2])
-            c_quant(r, 1)
-            c_bank(r, 3, ENG_C[r][3])
-            c_quant(r, 2)
-            h_bank(r, ENG_H[r])
-            c_quant(r, 3)
-            h_quant(r)
-
-        acc = {}
-
-        def s2(tt, nb, g):
-            if g == 0:
-                acc[(tt, nb)] = new_bank(F32)
-            cols = slice(P * tt, P * (tt + 1))
-            mx(acc[(tt, nb)][:], h_codes[g][:, cols], h_scales[g][:, cols], w2_codes[(g, nb)][:], w2_scales[(g, nb)][:], g == 0, g == 3)
-
-        sumsq = {}
-        scaled = {}
-        for tt in range(2):
-            sumsq[tt] = const.tile([P, 2], F32, name="sumsq%d" % tt)
-
-        def square(tt, nb):
-            junk = work.tile([P, 512], BF16, tag="junk", name="junk", bufs=2)
-            nc.scalar.activation(out=junk[:], in_=acc[(tt, nb)][:], func=AF.Square, scale=1.0 / 32.0, accum_out=sumsq[tt][:, nb : nb + 1])
-
-        def gain(tt, nb):
-            t = work.tile([P, 512], F32, name="scaled%d_%d" % (tt, nb), bufs=1)
-            nc.vector.tensor_tensor(out=t[:], in0=acc[(tt, nb)][:], in1=bc[("w", nb)][:], op=ALU.mult)
-            scaled[(tt, nb)] = t
-
-        rstd = {}
-
-        def inv_rms(tt):
-            ms = const.tile([P, 1], F32, name="ms%d" % tt)
-            nc.gpsimd.tensor_scalar(out=ms[:], in0=sumsq[tt][:, 0:1], scalar1=sumsq[tt][:, 1:2], scalar2=EPS, op0=ALU.add, op1=ALU.add)
-            rstd[tt] = const.tile([P, 1], F32, name="rstd%d" % tt)
-            nc.gpsimd.tensor_tensor(out=rstd[tt][:], in0=ms[:], in1=neghalf[:], op=ALU.pow)
-
-        def finish(tt, nb):
-            o = work.tile([P, 512], F32, name="o%d_%d" % (tt, nb), bufs=1)
-            nc.vector.scalar_tensor_tensor(out=o[:], in0=scaled[(tt, nb)][:], scalar=rstd[tt][:, 0:1], in1=bc[("b", nb)][:], op0=ALU.mult, op1=ALU.add)
-            nc.sync.dma_start(out=out[P * tt : P * (tt + 1), 512 * nb : 512 * (nb + 1)], in_=o[:])
-
-        for nb in range(2):
-            for g in range(3):
-                s2(0, nb, g)
-        s2(0, 0, 3)
-        s2(0, 1, 3)
-        for tt in range(2):
-            if tt == 1:
-                for nb in range(2):
-                    for g in range(4):
-                        s2(1, nb, g)
-            square(tt, 0)
-            square(tt, 1)
-            gain(tt, 0)
-            gain(tt, 1)
-            inv_rms(tt)
-            finish(tt, 0)
-            finish(tt, 1)
+        for tt in range(TOKEN_TILES):
+            sumsq = const.tile([P, OUT_BANKS], F32, name="sumsq%d" % tt)
+            scaled = []
+            for nb in range(OUT_BANKS):
+                acc = new_bank(F32)
+                for g in range(GROUPS):
+                    matmul_mx(acc[:], h_mx[g], slice(P * tt, P * (tt + 1)), w2_mx[(g, nb)], g == 0, g == GROUPS - 1)
+                junk = work.tile([P, N_BANK], BF16, tag="junk", name="junk", bufs=2)
+                nc.scalar.activation(out=junk[:], in_=acc[:], func=AF.Square, scale=D_OUT**-0.5, accum_out=sumsq[:, nb : nb + 1])
+                scaled.append(work.tile([P, N_BANK], F32, name="scaled%d_%d" % (tt, nb), bufs=1))
+                nc.vector.tensor_tensor(out=scaled[nb][:], in0=acc[:], in1=spread["norm_w"][:, N_BANK * nb : N_BANK * (nb + 1)], op=ALU.mult)
+            mean_sq = const.tile([P, 1], F32, name="mean_sq%d" % tt)
+            nc.gpsimd.tensor_scalar(out=mean_sq[:], in0=sumsq[:, 0:1], scalar1=sumsq[:, 1:2], scalar2=EPS, op0=ALU.add, op1=ALU.add)
+            rstd = const.tile([P, 1], F32, name="rstd%d" % tt)
+            nc.gpsimd.tensor_tensor(out=rstd[:], in0=mean_sq[:], in1=neghalf[:], op=ALU.pow)
+            for nb in range(OUT_BANKS):
+                result = work.tile([P, N_BANK], F32, name="result%d_%d" % (tt, nb), bufs=1)
+                nc.vector.scalar_tensor_tensor(out=result[:], in0=scaled[nb][:], scalar=rstd[:, 0:1], in1=bias[nb][:], op0=ALU.mult, op1=ALU.add)
+                nc.sync.dma_start(out=out[P * tt : P * (tt + 1), N_BANK * nb : N_BANK * (nb + 1)], in_=result[:])

from contextlib import ExitStack

import concourse.mybir as mybir
from concourse.masks import make_identity

F32 = mybir.dt.float32
BF16 = mybir.dt.bfloat16
U32 = mybir.dt.uint32
U8 = mybir.dt.uint8
FP8X4 = mybir.dt.float8_e4m3fn_x4
AF = mybir.ActivationFunctionType
ALU = mybir.AluOpType

TOKENS, K_IN, HIDDEN, D_OUT = 256, 512, 2048, 1024
EPS = 1e-05
FLOPS = 2 * TOKENS * K_IN * HIDDEN * 2 + 2 * TOKENS * HIDDEN * D_OUT

P = 128
K_PASS = 512
N_BANK = 512
WORDS = K_PASS // 2
GROUPS = HIDDEN // K_PASS
TOKEN_TILES = TOKENS // P
OUT_BANKS = D_OUT // N_BANK

FIRST_PRODUCT_PSUM = F32


def tile_observationembeddingv2_pa_kernel(tc, x0, w1_g0, w3_g0, w2_g0, norm_w, norm_b, term_embed0, out):
    nc = tc.nc
    with ExitStack() as ctx:
        const = ctx.enter_context(tc.tile_pool(name="const", bufs=1))
        raw = ctx.enter_context(tc.tile_pool(name="raw", bufs=1))
        grp = ctx.enter_context(tc.tile_pool(name="grp", bufs=4))
        mxp = ctx.enter_context(tc.tile_pool(name="mxp", bufs=1))
        work = ctx.enter_context(tc.tile_pool(name="work", bufs=4))
        psum = ctx.enter_context(tc.psum_pool(name="psum", bufs=8))
        ctx.enter_context(tc.manual_schedule())

        neghalf = const.tile([P, 1], F32, name="neghalf")
        nc.vector.memset(neghalf[:], -0.5)
        warm = const.tile([P, 1], F32, name="warm")
        nc.scalar.activation(out=warm[:], in_=neghalf[:], func=AF.Silu)
        ident = const.tile([P, P], F32, name="ident")
        make_identity(nc, ident[:])

        weights = {"w1": w1_g0, "w3": w3_g0}
        w13_words = {}
        for nm in ("w1", "w3"):
            rows = weights[nm][0:K_PASS, :].rearrange("(p j) k -> p j k", j=4)
            for half in range(2):
                t = raw.tile([P, 2 * K_IN], BF16, name="%s_raw0_%d" % (nm, half))
                nc.sync.dma_start(out=t[:].rearrange("p (j k) -> p j k", j=2), in_=rows[:, 2 * half : 2 * half + 2, :])
                w13_words[(nm, 0, half)] = t[:].bitcast(F32)
        x_raw = raw.tile([P, TOKEN_TILES * K_IN], BF16, name="x_raw")
        nc.sync.dma_start(out=x_raw[:].rearrange("p (t k) -> p t k", t=TOKEN_TILES), in_=x0.rearrange("(t p) k -> p t k", p=P))
        for g in range(1, GROUPS):
            for nm in ("w1", "w3"):
                t = raw.tile([P, 4 * K_IN], BF16, name="%s_raw%d" % (nm, g))
                nc.sync.dma_start(out=t[:], in_=weights[nm][K_PASS * g : K_PASS * (g + 1), :].rearrange("(p j) k -> p (j k)", j=4))
                for half in range(2):
                    w13_words[(nm, g, half)] = t[:].bitcast(F32)[:, 2 * WORDS * half : 2 * WORDS * (half + 1)]
        w2_words = []
        for i in range(D_OUT // P):
            t = raw.tile([P, HIDDEN], BF16, name="w2_raw%d" % i)
            nc.sync.dma_start(out=t[:], in_=w2_g0[P * i : P * (i + 1), :])
            w2_words.append(t[:].bitcast(F32))
        spread = {}
        for nm, vec in (("norm_w", norm_w), ("norm_b", norm_b), ("term", term_embed0)):
            spread[nm] = const.tile([P, D_OUT], BF16, name="spread_%s" % nm)
            nc.sync.dma_start(out=spread[nm][:], in_=vec.partition_broadcast(P))

        def new_bank(dtype):
            bank = psum.tile([P, N_BANK], dtype, tag="bank", name="bank")
            return bank

        emptied = []

        def empty_bank(dst, src):
            if len(emptied) % 4 == 3:
                nc.vector.tensor_copy(out=dst, in_=src)
            else:
                nc.scalar.copy(out=dst, in_=src)
            emptied.append(1)

        waiting = []

        def quantize_waiting():
            while len(waiting) > 0:
                grouped, codes, scales = waiting.pop(0)
                nc.vector.quantize_mx(out=codes.bitcast(FP8X4), scales=scales, in_=grouped)

        def turn(word_slices, grouped_words, order):
            bank = new_bank(F32)
            for s in range(4):
                nc.tensor.transpose(out=bank[:, P * s : P * (s + 1)], in_=word_slices[s], identity=ident[:])
            if order == "row major":
                empty_bank(grouped_words.rearrange("p (r s) -> p r s", s=4), bank[:].rearrange("p (s r) -> p r s", s=4))
            else:
                empty_bank(grouped_words.rearrange("p (c u) -> p c u", u=2), bank[:].rearrange("p (u c) -> p c u", u=2))
            quantize_waiting()

        def turn_pair(views, step, start, codes, scales, name):
            grouped = grp.tile([P, 4 * 2 * P], BF16, tag="g1024", name=name, align_bytes=64, bufs=6)
            if step == 2:
                slices = [views[t][:, start + u : start + WORDS : 2] for u in range(2) for t in range(2)]
            else:
                slices = [views[t][:, start + P * u : start + P * (u + 1)] for u in range(2) for t in range(2)]
            turn(slices, grouped[:].bitcast(F32), "column major")
            waiting.append((grouped[:], codes, scales))

        def matmul_mx(acc, lhs, lhs_cols, rhs, start, stop):
            nc.tensor.matmul_mx(
                out=acc,
                lhsT=lhs[0][:, lhs_cols].bitcast(FP8X4),
                lhsT_scale=lhs[1][:, lhs_cols],
                rhs=rhs[0][:].bitcast(FP8X4),
                rhs_scale=rhs[1][:],
                start=start,
                stop=stop,
            )

        def mx_tiles(width, name):
            codes = mxp.tile([P, width], U32, name="%s_codes" % name, align_bytes=64)
            scales = mxp.tile([P, width], U8, name="%s_scales" % name, align_bytes=64)
            return (codes, scales)

        x_mx = mx_tiles(TOKENS, "x")
        w13_mx = {}

        def turn_w13(g):
            for nm in ("w1", "w3"):
                grouped = grp.tile([P, 4 * N_BANK], BF16, tag="g2048", name="gw", align_bytes=64, bufs=4)
                for half in range(2):
                    words = w13_words[(nm, g, half)]
                    slices = [words[:, WORDS * e + u : WORDS * (e + 1) : 2] for e in range(2) for u in range(2)]
                    turn(slices, grouped[:, 2 * N_BANK * half : 2 * N_BANK * (half + 1)].bitcast(F32), "row major")
                w13_mx[(nm, g)] = mx_tiles(N_BANK, "%s_%d" % (nm, g))
                waiting.append((grouped[:], w13_mx[(nm, g)][0][:], w13_mx[(nm, g)][1][:]))

        turn_w13(0)
        xw = x_raw[:].bitcast(F32)
        turn_pair([xw[:, WORDS * t : WORDS * (t + 1)] for t in range(TOKEN_TILES)], 2, 0, x_mx[0][:], x_mx[1][:], "gx")
        for g in range(1, GROUPS):
            turn_w13(g)
        quantize_waiting()

        hidden = {}
        for g in range(GROUPS):
            banks = {}
            gates = {}
            for nm in ("w1", "w3"):
                for tt in range(TOKEN_TILES):
                    banks[(nm, tt)] = new_bank(FIRST_PRODUCT_PSUM)
                    matmul_mx(banks[(nm, tt)][:], x_mx, slice(P * tt, P * (tt + 1)), w13_mx[(nm, g)], True, True)
                for tt in range(TOKEN_TILES):
                    if nm == "w1":
                        gates[tt] = work.tile([P, N_BANK], F32, tag="gate", name="gate", bufs=4)
                        nc.scalar.activation(out=gates[tt][:], in_=banks[(nm, tt)][:], func=AF.Silu)
                    else:
                        hidden[(g, tt)] = work.tile([P, N_BANK], BF16, name="hid%d_%d" % (g, tt), bufs=1)
                        nc.vector.tensor_tensor(out=hidden[(g, tt)][:], in0=banks[(nm, tt)][:], in1=gates[tt][:], op=ALU.mult)

        h_mx = {}
        w2_mx = {}
        for g in range(GROUPS):
            for nb in range(OUT_BANKS):
                w2_mx[(g, nb)] = mx_tiles(N_BANK, "w2_%d_%d" % (g, nb))

        def turn_hidden(g):
            h_mx[g] = mx_tiles(TOKENS, "h_%d" % g)
            turn_pair([hidden[(g, tt)][:].bitcast(F32) for tt in range(TOKEN_TILES)], 1, 0, h_mx[g][0][:], h_mx[g][1][:], "gh")

        def turn_w2(q):
            cols = slice(2 * P * (q % 2), 2 * P * (q % 2 + 1))
            for g in range(GROUPS):
                dst = w2_mx[(g, q // 2)]
                turn_pair(w2_words[2 * q : 2 * q + 2], 2, WORDS * g, dst[0][:, cols], dst[1][:, cols], "g2")

        for g in range(GROUPS - 1):
            turn_hidden(g)
        turn_w2(0)
        turn_hidden(GROUPS - 1)
        for q in range(1, 4):
            turn_w2(q)
        quantize_waiting()

        bias = []
        for nb in range(OUT_BANKS):
            cols = slice(N_BANK * nb, N_BANK * (nb + 1))
            bias.append(const.tile([P, N_BANK], F32, name="bias%d" % nb))
            nc.vector.tensor_tensor(out=bias[nb][:], in0=spread["norm_b"][:, cols], in1=spread["term"][:, cols], op=ALU.add)

        for tt in range(TOKEN_TILES):
            sumsq = const.tile([P, OUT_BANKS], F32, name="sumsq%d" % tt)
            scaled = []
            for nb in range(OUT_BANKS):
                acc = new_bank(F32)
                for g in range(GROUPS):
                    matmul_mx(acc[:], h_mx[g], slice(P * tt, P * (tt + 1)), w2_mx[(g, nb)], g == 0, g == GROUPS - 1)
                junk = work.tile([P, N_BANK], BF16, tag="junk", name="junk", bufs=2)
                nc.scalar.activation(out=junk[:], in_=acc[:], func=AF.Square, scale=D_OUT**-0.5, accum_out=sumsq[:, nb : nb + 1])
                scaled.append(work.tile([P, N_BANK], F32, name="scaled%d_%d" % (tt, nb), bufs=1))
                nc.vector.tensor_tensor(out=scaled[nb][:], in0=acc[:], in1=spread["norm_w"][:, N_BANK * nb : N_BANK * (nb + 1)], op=ALU.mult)
            mean_sq = const.tile([P, 1], F32, name="mean_sq%d" % tt)
            nc.gpsimd.tensor_scalar(out=mean_sq[:], in0=sumsq[:, 0:1], scalar1=sumsq[:, 1:2], scalar2=EPS, op0=ALU.add, op1=ALU.add)
            rstd = const.tile([P, 1], F32, name="rstd%d" % tt)
            nc.gpsimd.tensor_tensor(out=rstd[:], in0=mean_sq[:], in1=neghalf[:], op=ALU.pow)
            for nb in range(OUT_BANKS):
                result = work.tile([P, N_BANK], F32, name="result%d_%d" % (tt, nb), bufs=1)
                nc.vector.scalar_tensor_tensor(out=result[:], in0=scaled[nb][:], scalar=rstd[:, 0:1], in1=bias[nb][:], op0=ALU.mult, op1=ALU.add)
                nc.sync.dma_start(out=out[P * tt : P * (tt + 1), N_BANK * nb : N_BANK * (nb + 1)], in_=result[:])
